import numpy as np
import ml_dtypes


def mxq(x, axis, fmt="e4m3"):
    dtype, down = {"e4m3": (ml_dtypes.float8_e4m3fn, 7), "e5m2": (ml_dtypes.float8_e5m2, 14)}[fmt]
    v = np.moveaxis(np.asarray(x, np.float32).astype(ml_dtypes.bfloat16).astype(np.float64), axis, -1)
    blocks = v.reshape(v.shape[:-1] + (-1, 32))
    amax = np.abs(blocks).max(-1, keepdims=True)
    byte = np.maximum(np.where(amax > 0, np.frexp(amax)[1] - 1 + 127, 0) - down, 1)
    scale = np.exp2(byte - 127.0)
    codes = (blocks / scale).astype(np.float32).astype(dtype).astype(np.float64)
    return np.moveaxis((codes * scale).reshape(v.shape), -1, axis)


WIDE = False


def mx_kscale(k):
    if not WIDE:
        return np.ones(k)
    levels = np.array([10, -10, 5, -5, 0])
    a = np.random.permutation(np.resize(levels, k // 512 * 4)).reshape(k // 512, 4)
    idx = np.arange(k)
    return np.exp2(a[idx // 512, idx % 128 // 32])


BF16 = ml_dtypes.bfloat16


def bf(x):
    return np.asarray(x, np.float32).astype(BF16)


def f64(x):
    return np.asarray(x).astype(np.float64)


B, C, D, T, H, W, P = 4, 512, 256, 8, 16, 16, 2
N = T * H * W
NP = T * (H // P) * (W // P)


def conv1x1(wq, b, xq):
    return ((wq @ xq) + b[None, :, None]).reshape(B, D, T, H, W)


def maxpool(v):
    return v.reshape(B, D, T, H // P, P, W // P, P).max(axis=(4, 6))


def setup_inputs():
    s = mx_kscale(C)
    a = 1.0 / np.sqrt(C) / s[None, :]
    return {"x": bf(np.random.standard_normal((B, C, T, H, W)) * s[None, :, None, None, None]),
            "g_w": bf(np.random.standard_normal((D, C)) * 0.15 * a),
            "g_b": bf(np.random.standard_normal(D) * 0.03),
            "theta_w": bf(np.random.standard_normal((D, C)) * 2.0 * a),
            "theta_b": bf(np.random.standard_normal(D) * 0.2),
            "phi_w": bf(np.random.standard_normal((D, C)) * a),
            "phi_b": bf(np.random.standard_normal(D) * 0.1)}


def reference(x, g_w, g_b, theta_w, theta_b, phi_w, phi_b):
    xq = mxq(f64(x).reshape(B, C, N), 1, "e4m3")
    g_x = maxpool(conv1x1(mxq(f64(g_w), 1, "e4m3"), f64(g_b), xq)).reshape(B, D, NP)
    theta_x = conv1x1(mxq(f64(theta_w), 1, "e4m3"), f64(theta_b), xq).reshape(B, D, N)
    phi_x = maxpool(conv1x1(mxq(f64(phi_w), 1, "e4m3"), f64(phi_b), xq)).reshape(B, D, NP)
    return g_x, theta_x, phi_x

@@ -1,0 +1,238 @@
+from contextlib import ExitStack
+
+import concourse.mybir as mybir
+from concourse.masks import make_identity
+
+F32 = mybir.dt.float32
+BF16 = mybir.dt.bfloat16
+U32 = mybir.dt.uint32
+U8 = mybir.dt.uint8
+FP8X4 = mybir.dt.float8_e4m3fn_x4
+
+P = 128
+PACK = 4
+BATCH = 4
+CHANNELS = P * PACK
+OUT_CHANNELS = 256
+HALVES = OUT_CHANNELS // P
+WIDTH = 16
+WINDOW = 2
+POSITIONS = 8 * 16 * WIDTH
+CHUNK = 512
+CHUNKS_PER_BATCH = POSITIONS // CHUNK
+CHUNKS = BATCH * CHUNKS_PER_BATCH
+POOLED = POSITIONS // (WINDOW * WINDOW)
+POOLED_CHUNK = CHUNK // (WINDOW * WINDOW)
+RUN = 4
+
+VECTOR_COLUMNS = 64
+SCALAR_COLUMNS = CHUNK - VECTOR_COLUMNS
+
+G, PHI, THETA = 0, 1, 2
+CONVS = (G, PHI, THETA)
+POOLED_CONVS = (G, PHI)
+NAMES = ("g", "phi", "theta")
+
+QUANTISE_LAG = 2
+POOL_LAG = 3
+THETA_LAG = 4
+
+FLOPS = 2 * 3 * OUT_CHANNELS * CHANNELS * BATCH * POSITIONS
+
+
+def tile_nonlocalblocknd_pa_t_kernel(
+    tc, x, g_w, g_b, theta_w, theta_b, phi_w, phi_b, out_0, out_1, out_2
+):
+    nc = tc.nc
+    weights = (g_w, phi_w, theta_w)
+    biases = (g_b, phi_b, theta_b)
+    outputs = (out_0, out_2, out_1)
+
+    with ExitStack() as ctx:
+        keep = ctx.enter_context(tc.tile_pool(name="keep", bufs=1))
+        stage = ctx.enter_context(tc.tile_pool(name="stage", bufs=4))
+        psum = ctx.enter_context(tc.psum_pool(name="psum", bufs=4))
+        ctx.enter_context(tc.manual_schedule())
+
+        identity = keep.tile([P, P], F32, name="identity")
+        bias_raw = [keep.tile([P, HALVES], BF16, name="bias_raw_%s" % n) for n in NAMES]
+        bias = keep.tile([P, len(CONVS), HALVES], F32, name="bias")
+        w_raw = [keep.tile([P, HALVES * CHANNELS], BF16, name="w_raw_%s" % n) for n in NAMES]
+        w_grouped = [
+            keep.tile([P, HALVES * P * PACK], BF16, name="w_grouped_%s" % n, align_bytes=64)
+            for n in NAMES
+        ]
+        w_codes = keep.tile([P, len(CONVS), HALVES * P], U32, name="w_codes", align_bytes=64)
+        w_scales = keep.tile([P, len(CONVS), HALVES * P], U8, name="w_scales", align_bytes=64)
+        x_first = [
+            keep.tile([P, PACK, CHUNK], BF16, name="x_first_%d" % c) for c in range(CHUNKS_PER_BATCH)
+        ]
+        x_whole = [
+            keep.tile([P, PACK, POSITIONS], BF16, name="x_whole_%d" % b) for b in range(1, BATCH)
+        ]
+        x_codes = keep.tile([P, CHUNKS, CHUNK], U32, name="x_codes", align_bytes=64)
+        x_scales = keep.tile([P, CHUNKS, CHUNK], U8, name="x_scales", align_bytes=64)
+
+        for v in CONVS:
+            nc.scalar.dma_start(
+                out=bias_raw[v][:], in_=biases[v].rearrange("(p m) -> p m", m=HALVES)
+            )
+
+        def load_weight(v):
+            nc.sync.dma_start(
+                out=w_raw[v][:], in_=weights[v].rearrange("(p m) k -> p (m k)", m=HALVES)
+            )
+
+        def x_view(b):
+            return x[b].rearrange("(p j) t h w -> p j (t h w)", j=PACK)
+
+        def chunk_columns(c):
+            return slice(c * CHUNK, (c + 1) * CHUNK)
+
+        for c in range(CHUNKS_PER_BATCH):
+            nc.sync.dma_start(out=x_first[c][:], in_=x_view(0)[:, :, chunk_columns(c)])
+            if c == 0:
+                load_weight(G)
+                load_weight(PHI)
+            if c == QUANTISE_LAG:
+                load_weight(THETA)
+        for b in range(1, BATCH):
+            nc.sync.dma_start(out=x_whole[b - 1][:], in_=x_view(b))
+
+        make_identity(nc, identity[:])
+        for v in CONVS:
+            nc.scalar.activation(
+                out=bias[:, v, :], in_=bias_raw[v][:], func=mybir.ActivationFunctionType.Identity
+            )
+
+        def prepare_weight(v):
+            words = w_raw[v][:].bitcast(F32).rearrange("p (m q u) -> p m u q", m=HALVES, u=2)
+            turned = psum.tile([P, HALVES, 2, P], F32, tag="pool_acc", bufs=5)
+            for m in range(HALVES):
+                for u in range(2):
+                    nc.tensor.transpose(turned[:, m, u, :], words[:, m, u, :], identity[:])
+            nc.vector.tensor_copy(
+                out=w_grouped[v][:].bitcast(F32).rearrange("q (m p u) -> q m p u", m=HALVES, u=2),
+                in_=turned[:].rearrange("q m u p -> q m p u"),
+            )
+            nc.vector.quantize_mx(
+                out=w_codes[:, v, :].bitcast(FP8X4), scales=w_scales[:, v, :], in_=w_grouped[v][:]
+            )
+
+        grouped_of = {}
+        acc_of = {}
+        pooled_of = {}
+
+        def regroup(i):
+            b, c = divmod(i, CHUNKS_PER_BATCH)
+            grouped = stage.tile([P, CHUNK, PACK], BF16, tag="grouped", align_bytes=64)
+            source = x_first[c][:] if b == 0 else x_whole[b - 1][:, :, chunk_columns(c)]
+            nc.scalar.copy(
+                out=grouped[:, :SCALAR_COLUMNS, :].rearrange("p (c i) j -> p c j i", i=RUN),
+                in_=source[:, :, :SCALAR_COLUMNS].rearrange("p j (c i) -> p c j i", i=RUN),
+            )
+            nc.vector.tensor_copy(
+                out=grouped[:, SCALAR_COLUMNS:, :].rearrange("p (c i) j -> p c j i", i=RUN),
+                in_=source[:, :, SCALAR_COLUMNS:].rearrange("p j (c i) -> p c j i", i=RUN),
+            )
+            grouped_of[i] = grouped
+
+        def quantise(i):
+            nc.vector.quantize_mx(
+                out=x_codes[:, i, :].bitcast(FP8X4),
+                scales=x_scales[:, i, :],
+                in_=grouped_of[i][:].rearrange("p n j -> p (n j)"),
+            )
+
+        def multiply(i, v, m):
+            half = slice(m * P, (m + 1) * P)
+            if v == THETA:
+                acc = psum.tile([P, CHUNK], F32, tag="theta_acc", bufs=3)
+            else:
+                acc = psum.tile([P, CHUNK], F32, tag="pool_acc", bufs=5)
+            nc.tensor.matmul_mx(
+                out=acc[:],
+                lhsT=w_codes[:, v, half].bitcast(FP8X4),
+                lhsT_scale=w_scales[:, v, half],
+                rhs=x_codes[:, i, :].bitcast(FP8X4),
+                rhs_scale=x_scales[:, i, :],
+                start=True,
+                stop=True,
+            )
+            acc_of[(v, m)] = acc
+
+        def out_view(v, b):
+            return outputs[v][b].rearrange("(p m) n -> p m n", m=HALVES)
+
+        def leave_theta(theta_sb, m):
+            nc.scalar.activation(
+                out=theta_sb[:, m, :],
+                in_=acc_of[(THETA, m)][:],
+                func=mybir.ActivationFunctionType.Identity,
+                bias=bias[:, THETA, m : m + 1],
+            )
+
+        def leave_pooled(i, v, m):
+            c = i % CHUNKS_PER_BATCH
+            nc.vector.tensor_reduce(
+                out=pooled_of[v][:, m, c * POOLED_CHUNK : (c + 1) * POOLED_CHUNK].rearrange(
+                    "p (a w) -> p a w", w=WIDTH // WINDOW
+                ),
+                in_=acc_of[(v, m)][:].rearrange(
+                    "p (a r w s) -> p a w r s", r=WINDOW, w=WIDTH // WINDOW, s=WINDOW
+                ),
+                axis=mybir.AxisListType.XY,
+                op=mybir.AluOpType.max,
+            )
+
+        def finish_pooled(b, v, m):
+            pooled = pooled_of[v]
+            nc.gpsimd.tensor_scalar(
+                out=pooled[:, m, :],
+                in0=pooled[:, m, :],
+                scalar1=1.0,
+                scalar2=bias[:, v, m : m + 1],
+                op0=mybir.AluOpType.mult,
+                op1=mybir.AluOpType.add,
+            )
+            nc.sync.dma_start(out=out_view(v, b)[:, m, :], in_=pooled[:, m, :])
+
+        def in_range(i):
+            return 0 <= i < CHUNKS
+
+        for step in range(CHUNKS + THETA_LAG):
+            if step == 1:
+                prepare_weight(G)
+                prepare_weight(PHI)
+
+            fresh, pooling, leaving = step - QUANTISE_LAG, step - POOL_LAG, step - THETA_LAG
+            if in_range(fresh):
+                quantise(fresh)
+
+            if in_range(leaving):
+                theta_sb = stage.tile([P, HALVES, CHUNK], F32, tag="theta_sb", bufs=8)
+            for m in range(HALVES):
+                if in_range(leaving):
+                    leave_theta(theta_sb, m)
+                if in_range(leaving + 1):
+                    multiply(leaving + 1, THETA, m)
+            if in_range(leaving):
+                b, c = divmod(leaving, CHUNKS_PER_BATCH)
+                nc.sync.dma_start(out=out_view(THETA, b)[:, :, chunk_columns(c)], in_=theta_sb[:])
+
+            for v in POOLED_CONVS:
+                if in_range(pooling) and pooling % CHUNKS_PER_BATCH == 0:
+                    pooled = stage.tile([P, HALVES, POOLED], F32, tag="pooled", bufs=4)
+                    pooled_of[v] = pooled
+                for m in range(HALVES):
+                    if in_range(pooling):
+                        leave_pooled(pooling, v, m)
+                    if in_range(fresh):
+                        multiply(fresh, v, m)
+                    if in_range(pooling) and pooling % CHUNKS_PER_BATCH == CHUNKS_PER_BATCH - 1:
+                        finish_pooled(pooling // CHUNKS_PER_BATCH, v, m)
+
+            if step == THETA_LAG - 2:
+                prepare_weight(THETA)
+            if in_range(step):
+                regroup(step)

@@ -8,6 +8,7 @@ BF16 = mybir.dt.bfloat16
 U32 = mybir.dt.uint32
 U8 = mybir.dt.uint8
 FP8X4 = mybir.dt.float8_e4m3fn_x4
+IDENTITY = mybir.ActivationFunctionType.Identity
 
 P = 128
 PACK = 4
@@ -25,8 +26,7 @@ POOLED = POSITIONS // (WINDOW * WINDOW)
 POOLED_CHUNK = CHUNK // (WINDOW * WINDOW)
 RUN = 4
 
-VECTOR_COLUMNS = 64
-SCALAR_COLUMNS = CHUNK - VECTOR_COLUMNS
+SCALAR_COLUMNS = 224
 
 G, PHI, THETA = 0, 1, 2
 CONVS = (G, PHI, THETA)
@@ -34,8 +34,7 @@ POOLED_CONVS = (G, PHI)
 NAMES = ("g", "phi", "theta")
 
 QUANTISE_LAG = 2
-POOL_LAG = 3
-THETA_LAG = 4
+LEAVE_LAG = 3
 
 FLOPS = 2 * 3 * OUT_CHANNELS * CHANNELS * BATCH * POSITIONS
 
@@ -50,7 +49,7 @@ def tile_nonlocalblocknd_pa_t_kernel(
 
     with ExitStack() as ctx:
         keep = ctx.enter_context(tc.tile_pool(name="keep", bufs=1))
-        stage = ctx.enter_context(tc.tile_pool(name="stage", bufs=4))
+        stage = ctx.enter_context(tc.tile_pool(name="stage", bufs=2))
         psum = ctx.enter_context(tc.psum_pool(name="psum", bufs=4))
         ctx.enter_context(tc.manual_schedule())
 
@@ -78,42 +77,40 @@ def tile_nonlocalblocknd_pa_t_kernel(
                 out=bias_raw[v][:], in_=biases[v].rearrange("(p m) -> p m", m=HALVES)
             )
 
-        def load_weight(v):
-            nc.sync.dma_start(
-                out=w_raw[v][:], in_=weights[v].rearrange("(p m) k -> p (m k)", m=HALVES)
-            )
-
         def x_view(b):
             return x[b].rearrange("(p j) t h w -> p j (t h w)", j=PACK)
 
         def chunk_columns(c):
             return slice(c * CHUNK, (c + 1) * CHUNK)
 
-        for c in range(CHUNKS_PER_BATCH):
+        nc.sync.dma_start(out=x_first[0][:], in_=x_view(0)[:, :, chunk_columns(0)])
+        for v in CONVS:
+            nc.sync.dma_start(
+                out=w_raw[v][:], in_=weights[v].rearrange("(p m) k -> p (m k)", m=HALVES)
+            )
+        for c in range(1, CHUNKS_PER_BATCH):
             nc.sync.dma_start(out=x_first[c][:], in_=x_view(0)[:, :, chunk_columns(c)])
-            if c == 0:
-                load_weight(G)
-                load_weight(PHI)
-            if c == QUANTISE_LAG:
-                load_weight(THETA)
         for b in range(1, BATCH):
             nc.sync.dma_start(out=x_whole[b - 1][:], in_=x_view(b))
 
         make_identity(nc, identity[:])
         for v in CONVS:
-            nc.scalar.activation(
-                out=bias[:, v, :], in_=bias_raw[v][:], func=mybir.ActivationFunctionType.Identity
-            )
+            nc.scalar.activation(out=bias[:, v, :], in_=bias_raw[v][:], func=IDENTITY)
 
-        def prepare_weight(v):
+        turned_of = {}
+
+        def transpose_weight(v):
             words = w_raw[v][:].bitcast(F32).rearrange("p (m q u) -> p m u q", m=HALVES, u=2)
             turned = psum.tile([P, HALVES, 2, P], F32, tag="pool_acc", bufs=5)
             for m in range(HALVES):
                 for u in range(2):
                     nc.tensor.transpose(turned[:, m, u, :], words[:, m, u, :], identity[:])
+            turned_of[v] = turned
+
+        def quantise_weight(v):
             nc.vector.tensor_copy(
                 out=w_grouped[v][:].bitcast(F32).rearrange("q (m p u) -> q m p u", m=HALVES, u=2),
-                in_=turned[:].rearrange("q m u p -> q m p u"),
+                in_=turned_of[v][:].rearrange("q m u p -> q m p u"),
             )
             nc.vector.quantize_mx(
                 out=w_codes[:, v, :].bitcast(FP8X4), scales=w_scales[:, v, :], in_=w_grouped[v][:]
@@ -131,9 +128,13 @@ def tile_nonlocalblocknd_pa_t_kernel(
                 out=grouped[:, :SCALAR_COLUMNS, :].rearrange("p (c i) j -> p c j i", i=RUN),
                 in_=source[:, :, :SCALAR_COLUMNS].rearrange("p j (c i) -> p c j i", i=RUN),
             )
-            nc.vector.tensor_copy(
-                out=grouped[:, SCALAR_COLUMNS:, :].rearrange("p (c i) j -> p c j i", i=RUN),
-                in_=source[:, :, SCALAR_COLUMNS:].rearrange("p j (c i) -> p c j i", i=RUN),
+            nc.gpsimd.tensor_scalar(
+                out=grouped[:, SCALAR_COLUMNS:, :],
+                in0=source[:, :, SCALAR_COLUMNS:].rearrange("p j n -> p n j"),
+                scalar1=1.0,
+                scalar2=0.0,
+                op0=mybir.AluOpType.mult,
+                op1=mybir.AluOpType.add,
             )
             grouped_of[i] = grouped
 
@@ -168,7 +169,7 @@ def tile_nonlocalblocknd_pa_t_kernel(
             nc.scalar.activation(
                 out=theta_sb[:, m, :],
                 in_=acc_of[(THETA, m)][:],
-                func=mybir.ActivationFunctionType.Identity,
+                func=IDENTITY,
                 bias=bias[:, THETA, m : m + 1],
             )
 
@@ -187,52 +188,51 @@ def tile_nonlocalblocknd_pa_t_kernel(
 
         def finish_pooled(b, v, m):
             pooled = pooled_of[v]
-            nc.gpsimd.tensor_scalar(
-                out=pooled[:, m, :],
-                in0=pooled[:, m, :],
-                scalar1=1.0,
-                scalar2=bias[:, v, m : m + 1],
-                op0=mybir.AluOpType.mult,
-                op1=mybir.AluOpType.add,
+            nc.scalar.activation(
+                out=pooled[:, m, :], in_=pooled[:, m, :], func=IDENTITY, bias=bias[:, v, m : m + 1]
             )
             nc.sync.dma_start(out=out_view(v, b)[:, m, :], in_=pooled[:, m, :])
 
         def in_range(i):
             return 0 <= i < CHUNKS
 
-        for step in range(CHUNKS + THETA_LAG):
-            if step == 1:
-                prepare_weight(G)
-                prepare_weight(PHI)
+        for v in CONVS:
+            transpose_weight(v)
 
-            fresh, pooling, leaving = step - QUANTISE_LAG, step - POOL_LAG, step - THETA_LAG
+        for step in range(CHUNKS + LEAVE_LAG):
+            fresh, leaving = step - QUANTISE_LAG, step - LEAVE_LAG
+            b, c = divmod(leaving, CHUNKS_PER_BATCH)
+
+            if step == 1:
+                quantise_weight(G)
+                quantise_weight(PHI)
             if in_range(fresh):
                 quantise(fresh)
+            if step == QUANTISE_LAG:
+                quantise_weight(THETA)
 
+            for v in POOLED_CONVS:
+                if in_range(leaving) and c == 0:
+                    pooled = stage.tile([P, HALVES, POOLED], F32, tag="pooled", bufs=4)
+                    pooled_of[v] = pooled
+                for m in range(HALVES):
+                    if in_range(leaving):
+                        leave_pooled(leaving, v, m)
+                    if in_range(fresh):
+                        multiply(fresh, v, m)
             if in_range(leaving):
                 theta_sb = stage.tile([P, HALVES, CHUNK], F32, tag="theta_sb", bufs=8)
             for m in range(HALVES):
                 if in_range(leaving):
                     leave_theta(theta_sb, m)
-                if in_range(leaving + 1):
-                    multiply(leaving + 1, THETA, m)
+                if in_range(fresh):
+                    multiply(fresh, THETA, m)
             if in_range(leaving):
-                b, c = divmod(leaving, CHUNKS_PER_BATCH)
                 nc.sync.dma_start(out=out_view(THETA, b)[:, :, chunk_columns(c)], in_=theta_sb[:])
 
-            for v in POOLED_CONVS:
-                if in_range(pooling) and pooling % CHUNKS_PER_BATCH == 0:
-                    pooled = stage.tile([P, HALVES, POOLED], F32, tag="pooled", bufs=4)
-                    pooled_of[v] = pooled
-                for m in range(HALVES):
-                    if in_range(pooling):
-                        leave_pooled(pooling, v, m)
-                    if in_range(fresh):
-                        multiply(fresh, v, m)
-                    if in_range(pooling) and pooling % CHUNKS_PER_BATCH == CHUNKS_PER_BATCH - 1:
-                        finish_pooled(pooling // CHUNKS_PER_BATCH, v, m)
-
-            if step == THETA_LAG - 2:
-                prepare_weight(THETA)
             if in_range(step):
                 regroup(step)
+            if in_range(leaving) and c == CHUNKS_PER_BATCH - 1:
+                for v in POOLED_CONVS:
+                    for m in range(HALVES):
+                        finish_pooled(b, v, m)

@@ -26,12 +26,12 @@ POOLED = POSITIONS // (WINDOW * WINDOW)
 POOLED_CHUNK = CHUNK // (WINDOW * WINDOW)
 RUN = 4
 
-SCALAR_COLUMNS = 224
+SCALAR_COLUMNS = 192
 
-G, PHI, THETA = 0, 1, 2
-CONVS = (G, PHI, THETA)
+THETA, G, PHI = 0, 1, 2
+CONVS = (THETA, G, PHI)
 POOLED_CONVS = (G, PHI)
-NAMES = ("g", "phi", "theta")
+NAMES = ("theta", "g", "phi")
 
 QUANTISE_LAG = 2
 LEAVE_LAG = 3
@@ -43,9 +43,9 @@ def tile_nonlocalblocknd_pa_t_kernel(
     tc, x, g_w, g_b, theta_w, theta_b, phi_w, phi_b, out_0, out_1, out_2
 ):
     nc = tc.nc
-    weights = (g_w, phi_w, theta_w)
-    biases = (g_b, phi_b, theta_b)
-    outputs = (out_0, out_2, out_1)
+    weights = (theta_w, g_w, phi_w)
+    biases = (theta_b, g_b, phi_b)
+    outputs = (out_1, out_0, out_2)
 
     with ExitStack() as ctx:
         keep = ctx.enter_context(tc.tile_pool(name="keep", bufs=1))
@@ -107,11 +107,13 @@ def tile_nonlocalblocknd_pa_t_kernel(
                     nc.tensor.transpose(turned[:, m, u, :], words[:, m, u, :], identity[:])
             turned_of[v] = turned
 
-        def quantise_weight(v):
-            nc.vector.tensor_copy(
+        def regroup_weight(v):
+            nc.scalar.copy(
                 out=w_grouped[v][:].bitcast(F32).rearrange("q (m p u) -> q m p u", m=HALVES, u=2),
                 in_=turned_of[v][:].rearrange("q m u p -> q m p u"),
             )
+
+        def quantise_weight(v):
             nc.vector.quantize_mx(
                 out=w_codes[:, v, :].bitcast(FP8X4), scales=w_scales[:, v, :], in_=w_grouped[v][:]
             )
@@ -204,22 +206,14 @@ def tile_nonlocalblocknd_pa_t_kernel(
             b, c = divmod(leaving, CHUNKS_PER_BATCH)
 
             if step == 1:
-                quantise_weight(G)
-                quantise_weight(PHI)
+                for v in CONVS:
+                    regroup_weight(v)
             if in_range(fresh):
                 quantise(fresh)
             if step == QUANTISE_LAG:
-                quantise_weight(THETA)
+                for v in CONVS:
+                    quantise_weight(v)
 
-            for v in POOLED_CONVS:
-                if in_range(leaving) and c == 0:
-                    pooled = stage.tile([P, HALVES, POOLED], F32, tag="pooled", bufs=4)
-                    pooled_of[v] = pooled
-                for m in range(HALVES):
-                    if in_range(leaving):
-                        leave_pooled(leaving, v, m)
-                    if in_range(fresh):
-                        multiply(fresh, v, m)
             if in_range(leaving):
                 theta_sb = stage.tile([P, HALVES, CHUNK], F32, tag="theta_sb", bufs=8)
             for m in range(HALVES):
@@ -229,6 +223,15 @@ def tile_nonlocalblocknd_pa_t_kernel(
                     multiply(fresh, THETA, m)
             if in_range(leaving):
                 nc.sync.dma_start(out=out_view(THETA, b)[:, :, chunk_columns(c)], in_=theta_sb[:])
+            for v in POOLED_CONVS:
+                if in_range(leaving) and c == 0:
+                    pooled = stage.tile([P, HALVES, POOLED], F32, tag="pooled", bufs=4)
+                    pooled_of[v] = pooled
+                for m in range(HALVES):
+                    if in_range(leaving):
+                        leave_pooled(leaving, v, m)
+                    if in_range(fresh):
+                        multiply(fresh, v, m)
 
             if in_range(step):
                 regroup(step)

@@ -49,7 +49,7 @@ def tile_nonlocalblocknd_pa_t_kernel(
 
     with ExitStack() as ctx:
         keep = ctx.enter_context(tc.tile_pool(name="keep", bufs=1))
-        stage = ctx.enter_context(tc.tile_pool(name="stage", bufs=2))
+        stage = ctx.enter_context(tc.tile_pool(name="stage", bufs=4))
         psum = ctx.enter_context(tc.psum_pool(name="psum", bufs=4))
         ctx.enter_context(tc.manual_schedule())
 

@@ -26,7 +26,7 @@ POOLED = POSITIONS // (WINDOW * WINDOW)
 POOLED_CHUNK = CHUNK // (WINDOW * WINDOW)
 RUN = 4
 
-SCALAR_COLUMNS = 192
+SCALAR_COLUMNS = 224
 
 THETA, G, PHI = 0, 1, 2
 CONVS = (THETA, G, PHI)
@@ -49,7 +49,7 @@ def tile_nonlocalblocknd_pa_t_kernel(
 
     with ExitStack() as ctx:
         keep = ctx.enter_context(tc.tile_pool(name="keep", bufs=1))
-        stage = ctx.enter_context(tc.tile_pool(name="stage", bufs=4))
+        stage = ctx.enter_context(tc.tile_pool(name="stage", bufs=2))
         psum = ctx.enter_context(tc.psum_pool(name="psum", bufs=4))
         ctx.enter_context(tc.manual_schedule())
 

@@ -27,14 +27,19 @@ POOLED_CHUNK = CHUNK // (WINDOW * WINDOW)
 RUN = 4
 
 SCALAR_COLUMNS = 224
+FIRST_SCALAR_COLUMNS = 160
 
 THETA, G, PHI = 0, 1, 2
 CONVS = (THETA, G, PHI)
 POOLED_CONVS = (G, PHI)
 NAMES = ("theta", "g", "phi")
 
-QUANTISE_LAG = 2
-LEAVE_LAG = 3
+REGROUP_AHEAD = 3
+
+PARTS = 2
+PART = POOLED // PARTS
+CHUNKS_PER_PART = CHUNKS_PER_BATCH // PARTS
+TASKS_PER_STEP = 2
 
 FLOPS = 2 * 3 * OUT_CHANNELS * CHANNELS * BATCH * POSITIONS
 
@@ -54,8 +59,8 @@ def tile_nonlocalblocknd_pa_t_kernel(
         ctx.enter_context(tc.manual_schedule())
 
         identity = keep.tile([P, P], F32, name="identity")
+        warm = keep.tile([P, 1], F32, name="warm")
         bias_raw = [keep.tile([P, HALVES], BF16, name="bias_raw_%s" % n) for n in NAMES]
-        bias = keep.tile([P, len(CONVS), HALVES], F32, name="bias")
         w_raw = [keep.tile([P, HALVES * CHANNELS], BF16, name="w_raw_%s" % n) for n in NAMES]
         w_grouped = [
             keep.tile([P, HALVES * P * PACK], BF16, name="w_grouped_%s" % n, align_bytes=64)
@@ -83,39 +88,54 @@ def tile_nonlocalblocknd_pa_t_kernel(
         def chunk_columns(c):
             return slice(c * CHUNK, (c + 1) * CHUNK)
 
-        nc.sync.dma_start(out=x_first[0][:], in_=x_view(0)[:, :, chunk_columns(0)])
-        for v in CONVS:
+        def load_weight(v):
             nc.sync.dma_start(
                 out=w_raw[v][:], in_=weights[v].rearrange("(p m) k -> p (m k)", m=HALVES)
             )
-        for c in range(1, CHUNKS_PER_BATCH):
+
+        def load_first(c):
             nc.sync.dma_start(out=x_first[c][:], in_=x_view(0)[:, :, chunk_columns(c)])
+
+        load_first(0)
+        load_weight(G)
+        load_weight(PHI)
+        load_first(1)
+        load_weight(THETA)
+        for c in range(2, CHUNKS_PER_BATCH):
+            load_first(c)
         for b in range(1, BATCH):
             nc.sync.dma_start(out=x_whole[b - 1][:], in_=x_view(b))
 
         make_identity(nc, identity[:])
-        for v in CONVS:
-            nc.scalar.activation(out=bias[:, v, :], in_=bias_raw[v][:], func=IDENTITY)
+        nc.vector.memset(warm[:], 0.0)
+        nc.scalar.activation(out=warm[:], in_=warm[:], func=IDENTITY)
 
         turned_of = {}
 
-        def transpose_weight(v):
+        def transpose_weight(v, m):
             words = w_raw[v][:].bitcast(F32).rearrange("p (m q u) -> p m u q", m=HALVES, u=2)
-            turned = psum.tile([P, HALVES, 2, P], F32, tag="pool_acc", bufs=5)
-            for m in range(HALVES):
-                for u in range(2):
-                    nc.tensor.transpose(turned[:, m, u, :], words[:, m, u, :], identity[:])
-            turned_of[v] = turned
+            if v == THETA:
+                turned = psum.tile([P, 2, P], F32, tag="theta_acc", bufs=3)
+            else:
+                turned = psum.tile([P, 2, P], F32, tag="pool_acc", bufs=5)
+            for u in range(2):
+                nc.tensor.transpose(turned[:, u, :], words[:, m, u, :], identity[:])
+            turned_of[(v, m)] = turned
 
-        def regroup_weight(v):
+        def regroup_weight(v, m):
             nc.scalar.copy(
-                out=w_grouped[v][:].bitcast(F32).rearrange("q (m p u) -> q m p u", m=HALVES, u=2),
-                in_=turned_of[v][:].rearrange("q m u p -> q m p u"),
+                out=w_grouped[v][:, m * P * PACK : (m + 1) * P * PACK]
+                .bitcast(F32)
+                .rearrange("q (p u) -> q p u", u=2),
+                in_=turned_of[(v, m)][:].rearrange("q u p -> q p u"),
             )
 
-        def quantise_weight(v):
+        def quantise_weight(v, m):
+            half = slice(m * P, (m + 1) * P)
             nc.vector.quantize_mx(
-                out=w_codes[:, v, :].bitcast(FP8X4), scales=w_scales[:, v, :], in_=w_grouped[v][:]
+                out=w_codes[:, v, half].bitcast(FP8X4),
+                scales=w_scales[:, v, half],
+                in_=w_grouped[v][:, m * P * PACK : (m + 1) * P * PACK],
             )
 
         grouped_of = {}
@@ -126,18 +146,23 @@ def tile_nonlocalblocknd_pa_t_kernel(
             b, c = divmod(i, CHUNKS_PER_BATCH)
             grouped = stage.tile([P, CHUNK, PACK], BF16, tag="grouped", align_bytes=64)
             source = x_first[c][:] if b == 0 else x_whole[b - 1][:, :, chunk_columns(c)]
+            split = FIRST_SCALAR_COLUMNS if i == 0 else SCALAR_COLUMNS
             nc.scalar.copy(
-                out=grouped[:, :SCALAR_COLUMNS, :].rearrange("p (c i) j -> p c j i", i=RUN),
-                in_=source[:, :, :SCALAR_COLUMNS].rearrange("p j (c i) -> p c j i", i=RUN),
+                out=grouped[:, :split, :].rearrange("p (c i) j -> p c j i", i=RUN),
+                in_=source[:, :, :split].rearrange("p j (c i) -> p c j i", i=RUN),
             )
-            nc.gpsimd.tensor_scalar(
-                out=grouped[:, SCALAR_COLUMNS:, :],
-                in0=source[:, :, SCALAR_COLUMNS:].rearrange("p j n -> p n j"),
-                scalar1=1.0,
-                scalar2=0.0,
-                op0=mybir.AluOpType.mult,
-                op1=mybir.AluOpType.add,
-            )
+            others = source[:, :, split:].rearrange("p j n -> p n j")
+            if i == 0:
+                nc.vector.tensor_copy(out=grouped[:, split:, :], in_=others)
+            else:
+                nc.gpsimd.tensor_scalar(
+                    out=grouped[:, split:, :],
+                    in0=others,
+                    scalar1=1.0,
+                    scalar2=0.0,
+                    op0=mybir.AluOpType.mult,
+                    op1=mybir.AluOpType.add,
+                )
             grouped_of[i] = grouped
 
         def quantise(i):
@@ -162,17 +187,17 @@ def tile_nonlocalblocknd_pa_t_kernel(
                 start=True,
                 stop=True,
             )
-            acc_of[(v, m)] = acc
+            acc_of[(i, v, m)] = acc
 
         def out_view(v, b):
             return outputs[v][b].rearrange("(p m) n -> p m n", m=HALVES)
 
-        def leave_theta(theta_sb, m):
+        def leave_theta(i, theta_sb, m):
             nc.scalar.activation(
                 out=theta_sb[:, m, :],
-                in_=acc_of[(THETA, m)][:],
+                in_=acc_of[(i, THETA, m)][:],
                 func=IDENTITY,
-                bias=bias[:, THETA, m : m + 1],
+                bias=bias_raw[THETA][:, m : m + 1],
             )
 
         def leave_pooled(i, v, m):
@@ -181,61 +206,82 @@ def tile_nonlocalblocknd_pa_t_kernel(
                 out=pooled_of[v][:, m, c * POOLED_CHUNK : (c + 1) * POOLED_CHUNK].rearrange(
                     "p (a w) -> p a w", w=WIDTH // WINDOW
                 ),
-                in_=acc_of[(v, m)][:].rearrange(
+                in_=acc_of[(i, v, m)][:].rearrange(
                     "p (a r w s) -> p a w r s", r=WINDOW, w=WIDTH // WINDOW, s=WINDOW
                 ),
                 axis=mybir.AxisListType.XY,
                 op=mybir.AluOpType.max,
             )
 
-        def finish_pooled(b, v, m):
-            pooled = pooled_of[v]
+        def finish_pooled(pooled, b, v, m, part):
+            columns = slice(part * PART, (part + 1) * PART)
             nc.scalar.activation(
-                out=pooled[:, m, :], in_=pooled[:, m, :], func=IDENTITY, bias=bias[:, v, m : m + 1]
+                out=pooled[:, m, columns],
+                in_=pooled[:, m, columns],
+                func=IDENTITY,
+                bias=bias_raw[v][:, m : m + 1],
             )
-            nc.sync.dma_start(out=out_view(v, b)[:, m, :], in_=pooled[:, m, :])
+            nc.sync.dma_start(out=out_view(v, b)[:, m, columns], in_=pooled[:, m, columns])
 
         def in_range(i):
             return 0 <= i < CHUNKS
 
-        for v in CONVS:
-            transpose_weight(v)
-
-        for step in range(CHUNKS + LEAVE_LAG):
-            fresh, leaving = step - QUANTISE_LAG, step - LEAVE_LAG
-            b, c = divmod(leaving, CHUNKS_PER_BATCH)
-
-            if step == 1:
-                for v in CONVS:
-                    regroup_weight(v)
-            if in_range(fresh):
-                quantise(fresh)
-            if step == QUANTISE_LAG:
-                for v in CONVS:
-                    quantise_weight(v)
-
-            if in_range(leaving):
-                theta_sb = stage.tile([P, HALVES, CHUNK], F32, tag="theta_sb", bufs=8)
+        for v in POOLED_CONVS:
             for m in range(HALVES):
-                if in_range(leaving):
-                    leave_theta(theta_sb, m)
-                if in_range(fresh):
-                    multiply(fresh, THETA, m)
-            if in_range(leaving):
-                nc.sync.dma_start(out=out_view(THETA, b)[:, :, chunk_columns(c)], in_=theta_sb[:])
-            for v in POOLED_CONVS:
-                if in_range(leaving) and c == 0:
+                transpose_weight(v, m)
+        regroup(0)
+        quantise(0)
+        for v in POOLED_CONVS:
+            for m in range(HALVES):
+                regroup_weight(v, m)
+                quantise_weight(v, m)
+                multiply(0, v, m)
+        regroup(1)
+        for m in range(HALVES):
+            transpose_weight(THETA, m)
+            regroup_weight(THETA, m)
+        regroup(2)
+
+        tasks = []
+        for leaving in range(CHUNKS):
+            fresh = leaving + 1
+            b, c = divmod(leaving, CHUNKS_PER_BATCH)
+            if c == 0:
+                for v in POOLED_CONVS:
                     pooled = stage.tile([P, HALVES, POOLED], F32, tag="pooled", bufs=4)
                     pooled_of[v] = pooled
-                for m in range(HALVES):
-                    if in_range(leaving):
-                        leave_pooled(leaving, v, m)
-                    if in_range(fresh):
-                        multiply(fresh, v, m)
 
-            if in_range(step):
-                regroup(step)
-            if in_range(leaving) and c == CHUNKS_PER_BATCH - 1:
+            for m in range(HALVES):
+                leave_pooled(leaving, G, m)
+            if in_range(fresh):
+                quantise(fresh)
+                multiply(fresh, G, 0)
+                multiply(fresh, G, 1)
+                multiply(fresh, PHI, 0)
+            if leaving == 0:
+                for m in range(HALVES):
+                    quantise_weight(THETA, m)
+                    multiply(0, THETA, m)
+            theta_sb = stage.tile([P, HALVES, CHUNK], F32, tag="theta_sb", bufs=8)
+            for m in range(HALVES):
+                leave_theta(leaving, theta_sb, m)
+            nc.sync.dma_start(out=out_view(THETA, b)[:, :, chunk_columns(c)], in_=theta_sb[:])
+            if in_range(fresh):
+                multiply(fresh, THETA, 0)
+            leave_pooled(leaving, PHI, 0)
+            if in_range(fresh):
+                multiply(fresh, PHI, 1)
+            leave_pooled(leaving, PHI, 1)
+            if in_range(fresh):
+                multiply(fresh, THETA, 1)
+
+            if in_range(leaving + REGROUP_AHEAD):
+                regroup(leaving + REGROUP_AHEAD)
+            if (c + 1) % CHUNKS_PER_PART == 0:
                 for v in POOLED_CONVS:
                     for m in range(HALVES):
-                        finish_pooled(b, v, m)
+                        tasks.append((pooled_of[v], b, v, m, c // CHUNKS_PER_PART))
+            due = len(tasks) if leaving == CHUNKS - 1 else TASKS_PER_STEP
+            for task in tasks[:due]:
+                finish_pooled(*task)
+            tasks = tasks[due:]

@@ -36,6 +36,8 @@ NAMES = ("theta", "g", "phi")
 
 REGROUP_AHEAD = 3
 
+WARM_UP = 8
+
 PARTS = 2
 PART = POOLED // PARTS
 CHUNKS_PER_PART = CHUNKS_PER_BATCH // PARTS
@@ -60,6 +62,7 @@ def tile_nonlocalblocknd_pa_t_kernel(
 
         identity = keep.tile([P, P], F32, name="identity")
         warm = keep.tile([P, 1], F32, name="warm")
+        zeros = keep.tile([P, CHUNK], BF16, name="zeros")
         bias_raw = [keep.tile([P, HALVES], BF16, name="bias_raw_%s" % n) for n in NAMES]
         w_raw = [keep.tile([P, HALVES * CHANNELS], BF16, name="w_raw_%s" % n) for n in NAMES]
         w_grouped = [
@@ -109,6 +112,10 @@ def tile_nonlocalblocknd_pa_t_kernel(
         make_identity(nc, identity[:])
         nc.vector.memset(warm[:], 0.0)
         nc.scalar.activation(out=warm[:], in_=warm[:], func=IDENTITY)
+        nc.vector.memset(zeros[:], 0.0)
+        idle = psum.tile([P, CHUNK], F32, tag="theta_acc", bufs=3)
+        for k in range(WARM_UP):
+            nc.tensor.matmul(out=idle[:], lhsT=zeros[:, :P], rhs=zeros[:], start=True, stop=True)
 
         turned_of = {}
 

@@ -27,7 +27,7 @@ POOLED_CHUNK = CHUNK // (WINDOW * WINDOW)
 RUN = 4
 
 SCALAR_COLUMNS = 224
-FIRST_SCALAR_COLUMNS = 160
+VECTOR_REGROUPS = 3
 
 THETA, G, PHI = 0, 1, 2
 CONVS = (THETA, G, PHI)
@@ -35,6 +35,8 @@ POOLED_CONVS = (G, PHI)
 NAMES = ("theta", "g", "phi")
 
 REGROUP_AHEAD = 3
+
+CHUNKED = 2
 
 WARM_UP = 8
 
@@ -72,10 +74,12 @@ def tile_nonlocalblocknd_pa_t_kernel(
         w_codes = keep.tile([P, len(CONVS), HALVES * P], U32, name="w_codes", align_bytes=64)
         w_scales = keep.tile([P, len(CONVS), HALVES * P], U8, name="w_scales", align_bytes=64)
         x_first = [
-            keep.tile([P, PACK, CHUNK], BF16, name="x_first_%d" % c) for c in range(CHUNKS_PER_BATCH)
+            keep.tile([P, PACK, CHUNK], BF16, name="x_first_%d" % i)
+            for i in range(CHUNKED * CHUNKS_PER_BATCH)
         ]
         x_whole = [
-            keep.tile([P, PACK, POSITIONS], BF16, name="x_whole_%d" % b) for b in range(1, BATCH)
+            keep.tile([P, PACK, POSITIONS], BF16, name="x_whole_%d" % b)
+            for b in range(CHUNKED, BATCH)
         ]
         x_codes = keep.tile([P, CHUNKS, CHUNK], U32, name="x_codes", align_bytes=64)
         x_scales = keep.tile([P, CHUNKS, CHUNK], U8, name="x_scales", align_bytes=64)
@@ -96,18 +100,19 @@ def tile_nonlocalblocknd_pa_t_kernel(
                 out=w_raw[v][:], in_=weights[v].rearrange("(p m) k -> p (m k)", m=HALVES)
             )
 
-        def load_first(c):
-            nc.sync.dma_start(out=x_first[c][:], in_=x_view(0)[:, :, chunk_columns(c)])
+        def load_first(i):
+            b, c = divmod(i, CHUNKS_PER_BATCH)
+            nc.sync.dma_start(out=x_first[i][:], in_=x_view(b)[:, :, chunk_columns(c)])
 
         load_first(0)
         load_weight(G)
         load_weight(PHI)
         load_first(1)
         load_weight(THETA)
-        for c in range(2, CHUNKS_PER_BATCH):
-            load_first(c)
-        for b in range(1, BATCH):
-            nc.sync.dma_start(out=x_whole[b - 1][:], in_=x_view(b))
+        for i in range(2, CHUNKED * CHUNKS_PER_BATCH):
+            load_first(i)
+        for b in range(CHUNKED, BATCH):
+            nc.sync.dma_start(out=x_whole[b - CHUNKED][:], in_=x_view(b))
 
         make_identity(nc, identity[:])
         nc.vector.memset(warm[:], 0.0)
@@ -152,14 +157,14 @@ def tile_nonlocalblocknd_pa_t_kernel(
         def regroup(i):
             b, c = divmod(i, CHUNKS_PER_BATCH)
             grouped = stage.tile([P, CHUNK, PACK], BF16, tag="grouped", align_bytes=64)
-            source = x_first[c][:] if b == 0 else x_whole[b - 1][:, :, chunk_columns(c)]
-            split = FIRST_SCALAR_COLUMNS if i == 0 else SCALAR_COLUMNS
+            source = x_first[i][:] if b < CHUNKED else x_whole[b - CHUNKED][:, :, chunk_columns(c)]
+            split = SCALAR_COLUMNS
             nc.scalar.copy(
                 out=grouped[:, :split, :].rearrange("p (c i) j -> p c j i", i=RUN),
                 in_=source[:, :, :split].rearrange("p j (c i) -> p c j i", i=RUN),
             )
             others = source[:, :, split:].rearrange("p j n -> p n j")
-            if i == 0:
+            if i < VECTOR_REGROUPS:
                 nc.vector.tensor_copy(out=grouped[:, split:, :], in_=others)
             else:
                 nc.gpsimd.tensor_scalar(
@@ -247,7 +252,6 @@ def tile_nonlocalblocknd_pa_t_kernel(
         for m in range(HALVES):
             transpose_weight(THETA, m)
             regroup_weight(THETA, m)
-        regroup(2)
 
         tasks = []
         for leaving in range(CHUNKS):
@@ -260,15 +264,16 @@ def tile_nonlocalblocknd_pa_t_kernel(
 
             for m in range(HALVES):
                 leave_pooled(leaving, G, m)
+            if leaving == 0:
+                for m in range(HALVES):
+                    quantise_weight(THETA, m)
+                    multiply(0, THETA, m)
+                regroup(2)
             if in_range(fresh):
                 quantise(fresh)
                 multiply(fresh, G, 0)
                 multiply(fresh, G, 1)
                 multiply(fresh, PHI, 0)
-            if leaving == 0:
-                for m in range(HALVES):
-                    quantise_weight(THETA, m)
-                    multiply(0, THETA, m)
             theta_sb = stage.tile([P, HALVES, CHUNK], F32, tag="theta_sb", bufs=8)
             for m in range(HALVES):
                 leave_theta(leaving, theta_sb, m)

@@ -28,6 +28,7 @@ RUN = 4
 
 SCALAR_COLUMNS = 224
 VECTOR_REGROUPS = 3
+START_SCALAR_COLUMNS = (160, 320, 512)
 
 THETA, G, PHI = 0, 1, 2
 CONVS = (THETA, G, PHI)
@@ -142,12 +143,12 @@ def tile_nonlocalblocknd_pa_t_kernel(
                 in_=turned_of[(v, m)][:].rearrange("q u p -> q p u"),
             )
 
-        def quantise_weight(v, m):
-            half = slice(m * P, (m + 1) * P)
+        def quantise_weight(v, m, halves=1):
+            columns = slice(m * P, (m + halves) * P)
             nc.vector.quantize_mx(
-                out=w_codes[:, v, half].bitcast(FP8X4),
-                scales=w_scales[:, v, half],
-                in_=w_grouped[v][:, m * P * PACK : (m + 1) * P * PACK],
+                out=w_codes[:, v, columns].bitcast(FP8X4),
+                scales=w_scales[:, v, columns],
+                in_=w_grouped[v][:, m * P * PACK : (m + halves) * P * PACK],
             )
 
         grouped_of = {}
@@ -158,13 +159,15 @@ def tile_nonlocalblocknd_pa_t_kernel(
             b, c = divmod(i, CHUNKS_PER_BATCH)
             grouped = stage.tile([P, CHUNK, PACK], BF16, tag="grouped", align_bytes=64)
             source = x_first[i][:] if b < CHUNKED else x_whole[b - CHUNKED][:, :, chunk_columns(c)]
-            split = SCALAR_COLUMNS
+            split = START_SCALAR_COLUMNS[i] if i < VECTOR_REGROUPS else SCALAR_COLUMNS
             nc.scalar.copy(
                 out=grouped[:, :split, :].rearrange("p (c i) j -> p c j i", i=RUN),
                 in_=source[:, :, :split].rearrange("p j (c i) -> p c j i", i=RUN),
             )
             others = source[:, :, split:].rearrange("p j n -> p n j")
-            if i < VECTOR_REGROUPS:
+            if split == CHUNK:
+                pass
+            elif i < VECTOR_REGROUPS:
                 nc.vector.tensor_copy(out=grouped[:, split:, :], in_=others)
             else:
                 nc.gpsimd.tensor_scalar(
@@ -252,6 +255,7 @@ def tile_nonlocalblocknd_pa_t_kernel(
         for m in range(HALVES):
             transpose_weight(THETA, m)
             regroup_weight(THETA, m)
+        regroup(2)
 
         tasks = []
         for leaving in range(CHUNKS):
@@ -264,16 +268,15 @@ def tile_nonlocalblocknd_pa_t_kernel(
 
             for m in range(HALVES):
                 leave_pooled(leaving, G, m)
-            if leaving == 0:
-                for m in range(HALVES):
-                    quantise_weight(THETA, m)
-                    multiply(0, THETA, m)
-                regroup(2)
             if in_range(fresh):
                 quantise(fresh)
                 multiply(fresh, G, 0)
                 multiply(fresh, G, 1)
                 multiply(fresh, PHI, 0)
+            if leaving == 0:
+                quantise_weight(THETA, 0, HALVES)
+                for m in range(HALVES):
+                    multiply(0, THETA, m)
             theta_sb = stage.tile([P, HALVES, CHUNK], F32, tag="theta_sb", bufs=8)
             for m in range(HALVES):
                 leave_theta(leaving, theta_sb, m)

@@ -37,7 +37,8 @@ NAMES = ("theta", "g", "phi")
 
 REGROUP_AHEAD = 3
 
-CHUNKED = 2
+LOAD_CHUNKS = (1, 2, 4, 4)
+THETA_CHUNKS = 2
 
 WARM_UP = 8
 
@@ -74,13 +75,12 @@ def tile_nonlocalblocknd_pa_t_kernel(
         ]
         w_codes = keep.tile([P, len(CONVS), HALVES * P], U32, name="w_codes", align_bytes=64)
         w_scales = keep.tile([P, len(CONVS), HALVES * P], U8, name="w_scales", align_bytes=64)
-        x_first = [
-            keep.tile([P, PACK, CHUNK], BF16, name="x_first_%d" % i)
-            for i in range(CHUNKED * CHUNKS_PER_BATCH)
-        ]
-        x_whole = [
-            keep.tile([P, PACK, POSITIONS], BF16, name="x_whole_%d" % b)
-            for b in range(CHUNKED, BATCH)
+        x_pieces = [
+            [
+                keep.tile([P, PACK, n * CHUNK], BF16, name="x_%d_%d" % (b, k))
+                for k in range(CHUNKS_PER_BATCH // n)
+            ]
+            for b, n in enumerate(LOAD_CHUNKS)
         ]
         x_codes = keep.tile([P, CHUNKS, CHUNK], U32, name="x_codes", align_bytes=64)
         x_scales = keep.tile([P, CHUNKS, CHUNK], U8, name="x_scales", align_bytes=64)
@@ -101,19 +101,20 @@ def tile_nonlocalblocknd_pa_t_kernel(
                 out=w_raw[v][:], in_=weights[v].rearrange("(p m) k -> p (m k)", m=HALVES)
             )
 
-        def load_first(i):
-            b, c = divmod(i, CHUNKS_PER_BATCH)
-            nc.sync.dma_start(out=x_first[i][:], in_=x_view(b)[:, :, chunk_columns(c)])
+        def load_piece(b, k):
+            width = LOAD_CHUNKS[b] * CHUNK
+            nc.sync.dma_start(
+                out=x_pieces[b][k][:], in_=x_view(b)[:, :, k * width : (k + 1) * width]
+            )
 
-        load_first(0)
+        load_piece(0, 0)
         load_weight(G)
         load_weight(PHI)
-        load_first(1)
+        load_piece(0, 1)
         load_weight(THETA)
-        for i in range(2, CHUNKED * CHUNKS_PER_BATCH):
-            load_first(i)
-        for b in range(CHUNKED, BATCH):
-            nc.sync.dma_start(out=x_whole[b - CHUNKED][:], in_=x_view(b))
+        for b in range(BATCH):
+            for k in range(2 if b == 0 else 0, len(x_pieces[b])):
+                load_piece(b, k)
 
         make_identity(nc, identity[:])
         nc.vector.memset(warm[:], 0.0)
@@ -158,7 +159,8 @@ def tile_nonlocalblocknd_pa_t_kernel(
         def regroup(i):
             b, c = divmod(i, CHUNKS_PER_BATCH)
             grouped = stage.tile([P, CHUNK, PACK], BF16, tag="grouped", align_bytes=64)
-            source = x_first[i][:] if b < CHUNKED else x_whole[b - CHUNKED][:, :, chunk_columns(c)]
+            k, c_in_piece = divmod(c, LOAD_CHUNKS[b])
+            source = x_pieces[b][k][:, :, chunk_columns(c_in_piece)]
             split = START_SCALAR_COLUMNS[i] if i < VECTOR_REGROUPS else SCALAR_COLUMNS
             nc.scalar.copy(
                 out=grouped[:, :split, :].rearrange("p (c i) j -> p c j i", i=RUN),
@@ -209,7 +211,7 @@ def tile_nonlocalblocknd_pa_t_kernel(
 
         def leave_theta(i, theta_sb, m):
             nc.scalar.activation(
-                out=theta_sb[:, m, :],
+                out=theta_sb[:, m, chunk_columns(i % THETA_CHUNKS)],
                 in_=acc_of[(i, THETA, m)][:],
                 func=IDENTITY,
                 bias=bias_raw[THETA][:, m : m + 1],
@@ -236,7 +238,12 @@ def tile_nonlocalblocknd_pa_t_kernel(
                 func=IDENTITY,
                 bias=bias_raw[v][:, m : m + 1],
             )
-            nc.sync.dma_start(out=out_view(v, b)[:, m, columns], in_=pooled[:, m, columns])
+            if m < HALVES - 1:
+                return
+            if b == BATCH - 1:
+                nc.sync.dma_start(out=out_view(v, b)[:, :, columns], in_=pooled[:, :, columns])
+            elif part == PARTS - 1:
+                nc.sync.dma_start(out=out_view(v, b), in_=pooled[:])
 
         def in_range(i):
             return 0 <= i < CHUNKS
@@ -277,10 +284,21 @@ def tile_nonlocalblocknd_pa_t_kernel(
                 quantise_weight(THETA, 0, HALVES)
                 for m in range(HALVES):
                     multiply(0, THETA, m)
-            theta_sb = stage.tile([P, HALVES, CHUNK], F32, tag="theta_sb", bufs=8)
+            last_ones = leaving >= CHUNKS - THETA_CHUNKS
+            if c % THETA_CHUNKS == 0:
+                theta_sb = stage.tile([P, HALVES, THETA_CHUNKS * CHUNK], F32, tag="theta_sb", bufs=4)
             for m in range(HALVES):
                 leave_theta(leaving, theta_sb, m)
-            nc.sync.dma_start(out=out_view(THETA, b)[:, :, chunk_columns(c)], in_=theta_sb[:])
+            if last_ones:
+                nc.sync.dma_start(
+                    out=out_view(THETA, b)[:, :, chunk_columns(c)],
+                    in_=theta_sb[:, :, chunk_columns(c % THETA_CHUNKS)],
+                )
+            elif (c + 1) % THETA_CHUNKS == 0:
+                first = (c + 1 - THETA_CHUNKS) * CHUNK
+                nc.sync.dma_start(
+                    out=out_view(THETA, b)[:, :, first : (c + 1) * CHUNK], in_=theta_sb[:]
+                )
             if in_range(fresh):
                 multiply(fresh, THETA, 0)
             leave_pooled(leaving, PHI, 0)

@@ -230,8 +230,8 @@ def tile_nonlocalblocknd_pa_t_kernel(
                 op=mybir.AluOpType.max,
             )
 
-        def finish_pooled(pooled, b, v, m, part):
-            columns = slice(part * PART, (part + 1) * PART)
+        def finish_pooled(pooled, b, v, m, first, end):
+            columns = slice(first, end)
             nc.scalar.activation(
                 out=pooled[:, m, columns],
                 in_=pooled[:, m, columns],
@@ -242,7 +242,7 @@ def tile_nonlocalblocknd_pa_t_kernel(
                 return
             if b == BATCH - 1:
                 nc.sync.dma_start(out=out_view(v, b)[:, :, columns], in_=pooled[:, :, columns])
-            elif part == PARTS - 1:
+            elif end == POOLED:
                 nc.sync.dma_start(out=out_view(v, b), in_=pooled[:])
 
         def in_range(i):
@@ -265,6 +265,7 @@ def tile_nonlocalblocknd_pa_t_kernel(
         regroup(2)
 
         tasks = []
+        done = 0
         for leaving in range(CHUNKS):
             fresh = leaving + 1
             b, c = divmod(leaving, CHUNKS_PER_BATCH)
@@ -289,12 +290,12 @@ def tile_nonlocalblocknd_pa_t_kernel(
                 theta_sb = stage.tile([P, HALVES, THETA_CHUNKS * CHUNK], F32, tag="theta_sb", bufs=4)
             for m in range(HALVES):
                 leave_theta(leaving, theta_sb, m)
-            if last_ones:
-                nc.sync.dma_start(
-                    out=out_view(THETA, b)[:, :, chunk_columns(c)],
-                    in_=theta_sb[:, :, chunk_columns(c % THETA_CHUNKS)],
-                )
-            elif (c + 1) % THETA_CHUNKS == 0:
+                if last_ones:
+                    nc.sync.dma_start(
+                        out=out_view(THETA, b)[:, m, chunk_columns(c)],
+                        in_=theta_sb[:, m, chunk_columns(c % THETA_CHUNKS)],
+                    )
+            if not last_ones and (c + 1) % THETA_CHUNKS == 0:
                 first = (c + 1 - THETA_CHUNKS) * CHUNK
                 nc.sync.dma_start(
                     out=out_view(THETA, b)[:, :, first : (c + 1) * CHUNK], in_=theta_sb[:]
@@ -310,11 +311,13 @@ def tile_nonlocalblocknd_pa_t_kernel(
 
             if in_range(leaving + REGROUP_AHEAD):
                 regroup(leaving + REGROUP_AHEAD)
-            if (c + 1) % CHUNKS_PER_PART == 0:
+            if (c + 1) % CHUNKS_PER_PART == 0 or last_ones:
+                end = (c + 1) * POOLED_CHUNK
                 for v in POOLED_CONVS:
                     for m in range(HALVES):
-                        tasks.append((pooled_of[v], b, v, m, c // CHUNKS_PER_PART))
-            due = len(tasks) if leaving == CHUNKS - 1 else TASKS_PER_STEP
+                        tasks.append((pooled_of[v], b, v, m, done, end))
+                done = end % POOLED
+            due = len(tasks) if last_ones else TASKS_PER_STEP
             for task in tasks[:due]:
                 finish_pooled(*task)
             tasks = tasks[due:]

@@ -26,7 +26,7 @@ POOLED = POSITIONS // (WINDOW * WINDOW)
 POOLED_CHUNK = CHUNK // (WINDOW * WINDOW)
 RUN = 4
 
-SCALAR_COLUMNS = 224
+SCALAR_COLUMNS = 192
 VECTOR_REGROUPS = 3
 START_SCALAR_COLUMNS = (160, 320, 512)
 

from contextlib import ExitStack

import concourse.mybir as mybir
from concourse.masks import make_identity

F32 = mybir.dt.float32
BF16 = mybir.dt.bfloat16
U32 = mybir.dt.uint32
U8 = mybir.dt.uint8
FP8X4 = mybir.dt.float8_e4m3fn_x4
IDENTITY = mybir.ActivationFunctionType.Identity

P = 128
PACK = 4
BATCH = 4
CHANNELS = P * PACK
OUT_CHANNELS = 256
HALVES = OUT_CHANNELS // P
WIDTH = 16
WINDOW = 2
POSITIONS = 8 * 16 * WIDTH
CHUNK = 512
CHUNKS_PER_BATCH = POSITIONS // CHUNK
CHUNKS = BATCH * CHUNKS_PER_BATCH
POOLED = POSITIONS // (WINDOW * WINDOW)
POOLED_CHUNK = CHUNK // (WINDOW * WINDOW)
RUN = 4

SCALAR_COLUMNS = 192
VECTOR_REGROUPS = 3
START_SCALAR_COLUMNS = (160, 320, 512)

THETA, G, PHI = 0, 1, 2
CONVS = (THETA, G, PHI)
POOLED_CONVS = (G, PHI)
NAMES = ("theta", "g", "phi")

REGROUP_AHEAD = 3

LOAD_CHUNKS = (1, 2, 4, 4)
THETA_CHUNKS = 2

WARM_UP = 8

PARTS = 2
PART = POOLED // PARTS
CHUNKS_PER_PART = CHUNKS_PER_BATCH // PARTS
TASKS_PER_STEP = 2

FLOPS = 2 * 3 * OUT_CHANNELS * CHANNELS * BATCH * POSITIONS


def tile_nonlocalblocknd_pa_t_kernel(
    tc, x, g_w, g_b, theta_w, theta_b, phi_w, phi_b, out_0, out_1, out_2
):
    nc = tc.nc
    weights = (theta_w, g_w, phi_w)
    biases = (theta_b, g_b, phi_b)
    outputs = (out_1, out_0, out_2)

    with ExitStack() as ctx:
        keep = ctx.enter_context(tc.tile_pool(name="keep", bufs=1))
        stage = ctx.enter_context(tc.tile_pool(name="stage", bufs=2))
        psum = ctx.enter_context(tc.psum_pool(name="psum", bufs=4))
        ctx.enter_context(tc.manual_schedule())

        identity = keep.tile([P, P], F32, name="identity")
        warm = keep.tile([P, 1], F32, name="warm")
        zeros = keep.tile([P, CHUNK], BF16, name="zeros")
        bias_raw = [keep.tile([P, HALVES], BF16, name="bias_raw_%s" % n) for n in NAMES]
        w_raw = [keep.tile([P, HALVES * CHANNELS], BF16, name="w_raw_%s" % n) for n in NAMES]
        w_grouped = [
            keep.tile([P, HALVES * P * PACK], BF16, name="w_grouped_%s" % n, align_bytes=64)
            for n in NAMES
        ]
        w_codes = keep.tile([P, len(CONVS), HALVES * P], U32, name="w_codes", align_bytes=64)
        w_scales = keep.tile([P, len(CONVS), HALVES * P], U8, name="w_scales", align_bytes=64)
        x_pieces = [
            [
                keep.tile([P, PACK, n * CHUNK], BF16, name="x_%d_%d" % (b, k))
                for k in range(CHUNKS_PER_BATCH // n)
            ]
            for b, n in enumerate(LOAD_CHUNKS)
        ]
        x_codes = keep.tile([P, CHUNKS, CHUNK], U32, name="x_codes", align_bytes=64)
        x_scales = keep.tile([P, CHUNKS, CHUNK], U8, name="x_scales", align_bytes=64)

        for v in CONVS:
            nc.scalar.dma_start(
                out=bias_raw[v][:], in_=biases[v].rearrange("(p m) -> p m", m=HALVES)
            )

        def x_view(b):
            return x[b].rearrange("(p j) t h w -> p j (t h w)", j=PACK)

        def chunk_columns(c):
            return slice(c * CHUNK, (c + 1) * CHUNK)

        def load_weight(v):
            nc.sync.dma_start(
                out=w_raw[v][:], in_=weights[v].rearrange("(p m) k -> p (m k)", m=HALVES)
            )

        def load_piece(b, k):
            width = LOAD_CHUNKS[b] * CHUNK
            nc.sync.dma_start(
                out=x_pieces[b][k][:], in_=x_view(b)[:, :, k * width : (k + 1) * width]
            )

        load_piece(0, 0)
        load_weight(G)
        load_weight(PHI)
        load_piece(0, 1)
        load_weight(THETA)
        for b in range(BATCH):
            for k in range(2 if b == 0 else 0, len(x_pieces[b])):
                load_piece(b, k)

        make_identity(nc, identity[:])
        nc.vector.memset(warm[:], 0.0)
        nc.scalar.activation(out=warm[:], in_=warm[:], func=IDENTITY)
        nc.vector.memset(zeros[:], 0.0)
        idle = psum.tile([P, CHUNK], F32, tag="theta_acc", bufs=3)
        for k in range(WARM_UP):
            nc.tensor.matmul(out=idle[:], lhsT=zeros[:, :P], rhs=zeros[:], start=True, stop=True)

        turned_of = {}

        def transpose_weight(v, m):
            words = w_raw[v][:].bitcast(F32).rearrange("p (m q u) -> p m u q", m=HALVES, u=2)
            if v == THETA:
                turned = psum.tile([P, 2, P], F32, tag="theta_acc", bufs=3)
            else:
                turned = psum.tile([P, 2, P], F32, tag="pool_acc", bufs=5)
            for u in range(2):
                nc.tensor.transpose(turned[:, u, :], words[:, m, u, :], identity[:])
            turned_of[(v, m)] = turned

        def regroup_weight(v, m):
            nc.scalar.copy(
                out=w_grouped[v][:, m * P * PACK : (m + 1) * P * PACK]
                .bitcast(F32)
                .rearrange("q (p u) -> q p u", u=2),
                in_=turned_of[(v, m)][:].rearrange("q u p -> q p u"),
            )

        def quantise_weight(v, m, halves=1):
            columns = slice(m * P, (m + halves) * P)
            nc.vector.quantize_mx(
                out=w_codes[:, v, columns].bitcast(FP8X4),
                scales=w_scales[:, v, columns],
                in_=w_grouped[v][:, m * P * PACK : (m + halves) * P * PACK],
            )

        grouped_of = {}
        acc_of = {}
        pooled_of = {}

        def regroup(i):
            b, c = divmod(i, CHUNKS_PER_BATCH)
            grouped = stage.tile([P, CHUNK, PACK], BF16, tag="grouped", align_bytes=64)
            k, c_in_piece = divmod(c, LOAD_CHUNKS[b])
            source = x_pieces[b][k][:, :, chunk_columns(c_in_piece)]
            split = START_SCALAR_COLUMNS[i] if i < VECTOR_REGROUPS else SCALAR_COLUMNS
            nc.scalar.copy(
                out=grouped[:, :split, :].rearrange("p (c i) j -> p c j i", i=RUN),
                in_=source[:, :, :split].rearrange("p j (c i) -> p c j i", i=RUN),
            )
            others = source[:, :, split:].rearrange("p j n -> p n j")
            if split == CHUNK:
                pass
            elif i < VECTOR_REGROUPS:
                nc.vector.tensor_copy(out=grouped[:, split:, :], in_=others)
            else:
                nc.gpsimd.tensor_scalar(
                    out=grouped[:, split:, :],
                    in0=others,
                    scalar1=1.0,
                    scalar2=0.0,
                    op0=mybir.AluOpType.mult,
                    op1=mybir.AluOpType.add,
                )
            grouped_of[i] = grouped

        def quantise(i):
            nc.vector.quantize_mx(
                out=x_codes[:, i, :].bitcast(FP8X4),
                scales=x_scales[:, i, :],
                in_=grouped_of[i][:].rearrange("p n j -> p (n j)"),
            )

        def multiply(i, v, m):
            half = slice(m * P, (m + 1) * P)
            if v == THETA:
                acc = psum.tile([P, CHUNK], F32, tag="theta_acc", bufs=3)
            else:
                acc = psum.tile([P, CHUNK], F32, tag="pool_acc", bufs=5)
            nc.tensor.matmul_mx(
                out=acc[:],
                lhsT=w_codes[:, v, half].bitcast(FP8X4),
                lhsT_scale=w_scales[:, v, half],
                rhs=x_codes[:, i, :].bitcast(FP8X4),
                rhs_scale=x_scales[:, i, :],
                start=True,
                stop=True,
            )
            acc_of[(i, v, m)] = acc

        def out_view(v, b):
            return outputs[v][b].rearrange("(p m) n -> p m n", m=HALVES)

        def leave_theta(i, theta_sb, m):
            nc.scalar.activation(
                out=theta_sb[:, m, chunk_columns(i % THETA_CHUNKS)],
                in_=acc_of[(i, THETA, m)][:],
                func=IDENTITY,
                bias=bias_raw[THETA][:, m : m + 1],
            )

        def leave_pooled(i, v, m):
            c = i % CHUNKS_PER_BATCH
            nc.vector.tensor_reduce(
                out=pooled_of[v][:, m, c * POOLED_CHUNK : (c + 1) * POOLED_CHUNK].rearrange(
                    "p (a w) -> p a w", w=WIDTH // WINDOW
                ),
                in_=acc_of[(i, v, m)][:].rearrange(
                    "p (a r w s) -> p a w r s", r=WINDOW, w=WIDTH // WINDOW, s=WINDOW
                ),
                axis=mybir.AxisListType.XY,
                op=mybir.AluOpType.max,
            )

        def finish_pooled(pooled, b, v, m, first, end):
            columns = slice(first, end)
            nc.scalar.activation(
                out=pooled[:, m, columns],
                in_=pooled[:, m, columns],
                func=IDENTITY,
                bias=bias_raw[v][:, m : m + 1],
            )
            if m < HALVES - 1:
                return
            if b == BATCH - 1:
                nc.sync.dma_start(out=out_view(v, b)[:, :, columns], in_=pooled[:, :, columns])
            elif end == POOLED:
                nc.sync.dma_start(out=out_view(v, b), in_=pooled[:])

        def in_range(i):
            return 0 <= i < CHUNKS

        for v in POOLED_CONVS:
            for m in range(HALVES):
                transpose_weight(v, m)
        regroup(0)
        quantise(0)
        for v in POOLED_CONVS:
            for m in range(HALVES):
                regroup_weight(v, m)
                quantise_weight(v, m)
                multiply(0, v, m)
        regroup(1)
        for m in range(HALVES):
            transpose_weight(THETA, m)
            regroup_weight(THETA, m)
        regroup(2)

        tasks = []
        done = 0
        for leaving in range(CHUNKS):
            fresh = leaving + 1
            b, c = divmod(leaving, CHUNKS_PER_BATCH)
            if c == 0:
                for v in POOLED_CONVS:
                    pooled = stage.tile([P, HALVES, POOLED], F32, tag="pooled", bufs=4)
                    pooled_of[v] = pooled

            for m in range(HALVES):
                leave_pooled(leaving, G, m)
            if in_range(fresh):
                quantise(fresh)
                multiply(fresh, G, 0)
                multiply(fresh, G, 1)
                multiply(fresh, PHI, 0)
            if leaving == 0:
                quantise_weight(THETA, 0, HALVES)
                for m in range(HALVES):
                    multiply(0, THETA, m)
            last_ones = leaving >= CHUNKS - THETA_CHUNKS
            if c % THETA_CHUNKS == 0:
                theta_sb = stage.tile([P, HALVES, THETA_CHUNKS * CHUNK], F32, tag="theta_sb", bufs=4)
            for m in range(HALVES):
                leave_theta(leaving, theta_sb, m)
                if last_ones:
                    nc.sync.dma_start(
                        out=out_view(THETA, b)[:, m, chunk_columns(c)],
                        in_=theta_sb[:, m, chunk_columns(c % THETA_CHUNKS)],
                    )
            if not last_ones and (c + 1) % THETA_CHUNKS == 0:
                first = (c + 1 - THETA_CHUNKS) * CHUNK
                nc.sync.dma_start(
                    out=out_view(THETA, b)[:, :, first : (c + 1) * CHUNK], in_=theta_sb[:]
                )
            if in_range(fresh):
                multiply(fresh, THETA, 0)
            leave_pooled(leaving, PHI, 0)
            if in_range(fresh):
                multiply(fresh, PHI, 1)
            leave_pooled(leaving, PHI, 1)
            if in_range(fresh):
                multiply(fresh, THETA, 1)

            if in_range(leaving + REGROUP_AHEAD):
                regroup(leaving + REGROUP_AHEAD)
            if (c + 1) % CHUNKS_PER_PART == 0 or last_ones:
                end = (c + 1) * POOLED_CHUNK
                for v in POOLED_CONVS:
                    for m in range(HALVES):
                        tasks.append((pooled_of[v], b, v, m, done, end))
                done = end % POOLED
            due = len(tasks) if last_ones else TASKS_PER_STEP
            for task in tasks[:due]:
                finish_pooled(*task)
            tasks = tasks[due:]
